import numpy as np
import ml_dtypes


def mxq(x, axis, fmt="e4m3"):
    dtype, down = {"e4m3": (ml_dtypes.float8_e4m3fn, 7), "e5m2": (ml_dtypes.float8_e5m2, 14)}[fmt]
    v = np.moveaxis(np.asarray(x, np.float32).astype(ml_dtypes.bfloat16).astype(np.float64), axis, -1)
    blocks = v.reshape(v.shape[:-1] + (-1, 32))
    amax = np.abs(blocks).max(-1, keepdims=True)
    byte = np.maximum(np.where(amax > 0, np.frexp(amax)[1] - 1 + 127, 0) - down, 1)
    scale = np.exp2(byte - 127.0)
    codes = (blocks / scale).astype(np.float32).astype(dtype).astype(np.float64)
    return np.moveaxis((codes * scale).reshape(v.shape), -1, axis)


WIDE = False


def mx_kscale(k):
    if not WIDE:
        return np.ones(k)
    levels = np.array([10, -10, 5, -5, 0])
    a = np.random.permutation(np.resize(levels, k // 512 * 4)).reshape(k // 512, 4)
    idx = np.arange(k)
    return np.exp2(a[idx // 512, idx % 128 // 32])


BF16 = ml_dtypes.bfloat16


def bf(x):
    return np.asarray(x, np.float32).astype(BF16)


def f64(x):
    return np.asarray(x).astype(np.float64)


N, IN_F, OUT_F = 512, 1024, 128
POW = 2


def setup_inputs():
    s = mx_kscale(IN_F)
    u = np.exp2(np.round(np.log2(mx_kscale(N)) / 2))
    return {"input": bf(np.random.standard_normal((N, IN_F)) * s / (u * u)[:, None]),
            "adj": bf(np.random.uniform(0.0, 1.0, (N, N)) * 1.5 / N ** 0.25 * u),
            "weight": bf(np.random.uniform(-1.0, 1.0, (IN_F, OUT_F)) * 1.7 / np.sqrt(IN_F) / s[:, None]),
            "bias": bf(np.random.standard_normal(OUT_F) * 0.3)}


def reference(input, adj, weight, bias):
    k_adj = f64(adj) ** POW
    support = mxq(f64(input), 1, "e4m3") @ mxq(f64(weight), 0, "e4m3")
    out = (mxq(k_adj, 1, "e4m3") @ mxq(support, 0, "e4m3")) + f64(bias)
    return np.where(out > 0, out, np.expm1(out))

@@ -1,0 +1,202 @@
+from contextlib import ExitStack
+
+import concourse.mybir as mybir
+from concourse.masks import make_identity
+
+F32 = mybir.dt.float32
+BF16 = mybir.dt.bfloat16
+U32 = mybir.dt.uint32
+U8 = mybir.dt.uint8
+FP8X4 = mybir.dt.float8_e4m3fn_x4
+ACT = mybir.ActivationFunctionType
+ALU = mybir.AluOpType
+
+P = 128
+PACK = 4
+HALVES = 2
+PAIR = 2
+NODES = 512
+IN_F = 1024
+OUT_F = 128
+K_PASS = P * PACK
+PASSES = IN_F // K_PASS
+TILES = NODES // P
+
+FLOPS = 2 * NODES * IN_F * OUT_F + 2 * NODES * NODES * OUT_F
+
+
+def tile_netgraphconvolution_s_kernel(tc, x, adj, weight, bias, out):
+    nc = tc.nc
+    with ExitStack() as ctx:
+        keep = ctx.enter_context(tc.tile_pool(name="keep", bufs=1))
+        turned = ctx.enter_context(tc.psum_pool(name="turned", bufs=4))
+        sums = ctx.enter_context(tc.psum_pool(name="sums", bufs=1))
+        ctx.enter_context(tc.manual_schedule())
+
+        ident = keep.tile([P, P], F32)
+        make_identity(nc, ident[:])
+        warm_in = keep.tile([P, 1], F32)
+        warm_out = keep.tile([P, 1], F32)
+        nc.vector.memset(warm_in[:], 0.0)
+        bias_rows = keep.tile([P, OUT_F], BF16)
+        nc.vector.memset(bias_rows[:], 0.0)
+        ones = keep.tile([P, P], BF16)
+        nc.vector.memset(ones[:], 1.0)
+        nc.scalar.dma_start(out=bias_rows[0:1, :], in_=bias.rearrange("(o f) -> o f", o=1))
+        nc.scalar.activation(out=warm_out[:], in_=warm_in[:], func=ACT.Exp)
+
+        x_tiles = x.rearrange("(u p e) k -> u e p k", u=HALVES, p=P)
+        x_rows = []
+        for t in range(TILES):
+            x_t = keep.tile([P, IN_F], BF16, name="x_rows%d" % t)
+            x_rows.append(x_t)
+        nc.sync.dma_start(out=x_rows[0][:], in_=x_tiles[0, 0])
+        w_raw = keep.tile([P, PASSES, PACK, OUT_F], BF16)
+        nc.sync.dma_start(
+            out=w_raw[:].rearrange("p g (u e) c -> p (g u) (e c)", u=HALVES),
+            in_=weight.rearrange("(g u p e) c -> p (g u) (e c)", g=PASSES, u=HALVES, p=P),
+        )
+        for t in range(1, TILES):
+            nc.sync.dma_start(out=x_rows[t][:], in_=x_tiles[t // PAIR, t % PAIR])
+        adj_blocks = adj.rearrange("(p b) j -> p b j", b=TILES)
+        adj_rows = []
+        for h in range(TILES // PAIR):
+            adj_h = keep.tile([P, PAIR, NODES], BF16, name="adj_rows%d" % h)
+            nc.sync.dma_start(out=adj_h[:], in_=adj_blocks[:, PAIR * h : PAIR * h + PAIR, :])
+            adj_rows.append(adj_h)
+
+        w_grouped = keep.tile([P, PASSES, OUT_F, PACK], BF16, align_bytes=64)
+        nc.vector.tensor_copy(out=w_grouped[:], in_=w_raw[:].rearrange("p g t c -> p g c t"))
+        w_codes = keep.tile([P, PASSES, OUT_F], U32, align_bytes=64)
+        w_scales = keep.tile([P, PASSES, OUT_F], U8, align_bytes=64)
+        nc.vector.quantize_mx(
+            out=w_codes[:].rearrange("p g c -> p (g c)").bitcast(FP8X4),
+            scales=w_scales[:].rearrange("p g c -> p (g c)"),
+            in_=w_grouped[:].rearrange("p g c t -> p (g c t)"),
+        )
+
+        x_codes = keep.tile([P, TILES, PASSES, P], U32, align_bytes=64)
+        x_scales = keep.tile([P, TILES, PASSES, P], U8, align_bytes=64)
+        x_grouped = []
+        for t in range(TILES):
+            x_g = keep.tile([P, PASSES * P * PACK], BF16, name="x_grouped%d" % t, align_bytes=64)
+            x_grouped.append(x_g)
+
+        def turn_x(t):
+            x_words = x_rows[t][:].bitcast(F32)
+            xT = turned.tile([P, PASSES * HALVES, P], F32, tag="turned")
+            for q in range(PASSES * HALVES):
+                nc.tensor.transpose(xT[:, q, :], x_words[:, P * q : P * q + P], ident[:])
+            grouped_words = x_grouped[t][:].bitcast(F32).rearrange("p (g n u) -> p g n u", g=PASSES, u=HALVES)
+            turned_words = xT[:].rearrange("p (g u) n -> p g n u", g=PASSES)
+            if t % 2 == 0:
+                nc.scalar.copy(out=grouped_words, in_=turned_words)
+            else:
+                nc.vector.tensor_copy(out=grouped_words, in_=turned_words)
+
+        def quantise_x(t):
+            nc.vector.quantize_mx(
+                out=x_codes[:, t].rearrange("p g n -> p (g n)").bitcast(FP8X4),
+                scales=x_scales[:, t].rearrange("p g n -> p (g n)"),
+                in_=x_grouped[t][:],
+            )
+
+        turn_x(0)
+        for t in range(1, TILES):
+            turn_x(t)
+            quantise_x(t - 1)
+        quantise_x(TILES - 1)
+
+        a_codes = keep.tile([P, TILES, P], U32, align_bytes=64)
+        a_scales = keep.tile([P, TILES, P], U8, align_bytes=64)
+        adj_turned = []
+        for h in range(TILES // PAIR):
+            aT = turned.tile([P, PAIR, HALVES, P], F32, tag="turned")
+            for s in range(PAIR):
+                adj_words = adj_rows[h][:, s, :].bitcast(F32)
+                for u in range(HALVES):
+                    nc.tensor.transpose(aT[:, s, u, :], adj_words[:, P * u : P * u + P], ident[:])
+            adj_turned.append(aT)
+
+        def square_and_quantise(h):
+            a_grouped = keep.tile([P, PAIR, P * PACK], BF16, name="a_grouped%d" % h, align_bytes=64)
+            for s in range(PAIR):
+                nc.scalar.activation(
+                    out=a_grouped[:, s, :].rearrange("p (i u e) -> p i u e", u=HALVES, e=PAIR),
+                    in_=adj_turned[h][:, s].bitcast(BF16).rearrange("p u (i e) -> p i u e", e=PAIR),
+                    func=ACT.Square,
+                )
+            nc.vector.quantize_mx(
+                out=a_codes[:, PAIR * h : PAIR * h + PAIR, :].rearrange("p s i -> p (s i)").bitcast(FP8X4),
+                scales=a_scales[:, PAIR * h : PAIR * h + PAIR, :].rearrange("p s i -> p (s i)"),
+                in_=a_grouped[:].rearrange("p s c -> p (s c)"),
+            )
+
+        bias_ps = sums.tile([P, OUT_F], F32)
+        nc.tensor.matmul(out=bias_ps[:], lhsT=ones[:], rhs=bias_rows[:], start=True, stop=True)
+        bias_all = keep.tile([P, OUT_F], F32)
+
+        square_and_quantise(0)
+
+        sup_ps = sums.tile([P, TILES, OUT_F], F32)
+        for t in range(TILES):
+            for g in range(PASSES):
+                nc.tensor.matmul_mx(
+                    out=sup_ps[:, t, :],
+                    lhsT=x_codes[:, t, g, :].bitcast(FP8X4),
+                    lhsT_scale=x_scales[:, t, g, :],
+                    rhs=w_codes[:, g, :].bitcast(FP8X4),
+                    rhs_scale=w_scales[:, g, :],
+                    start=(g == 0),
+                    stop=(g == PASSES - 1),
+                )
+        sup_grouped = keep.tile([P, OUT_F, PACK], BF16, align_bytes=64)
+        nc.vector.tensor_copy(out=sup_grouped[:], in_=sup_ps[:].rearrange("p t f -> p f t"))
+        sup_codes = keep.tile([P, OUT_F], U32, align_bytes=64)
+        sup_scales = keep.tile([P, OUT_F], U8, align_bytes=64)
+        nc.vector.quantize_mx(
+            out=sup_codes[:].bitcast(FP8X4),
+            scales=sup_scales[:],
+            in_=sup_grouped[:].rearrange("p f t -> p (f t)"),
+        )
+
+        square_and_quantise(1)
+        nc.scalar.copy(out=bias_all[:], in_=bias_ps[:])
+
+        out_blocks = out.rearrange("(p b) f -> p b f", b=TILES)
+        z = []
+        e = []
+        for h in range(TILES // PAIR):
+            out_ps = sums.tile([P, PAIR, OUT_F], F32, name="out_ps%d" % h)
+            for s in range(PAIR):
+                b = PAIR * h + s
+                nc.tensor.matmul_mx(
+                    out=out_ps[:, s, :],
+                    lhsT=a_codes[:, b, :].bitcast(FP8X4),
+                    lhsT_scale=a_scales[:, b, :],
+                    rhs=sup_codes[:].bitcast(FP8X4),
+                    rhs_scale=sup_scales[:],
+                    start=True,
+                    stop=True,
+                )
+            z_h = keep.tile([P, PAIR, OUT_F], F32, name="z%d" % h)
+            nc.vector.tensor_tensor(
+                out=z_h[:], in0=out_ps[:], in1=bias_all[:].unsqueeze(1).to_broadcast([P, PAIR, OUT_F]), op=ALU.add
+            )
+            e_h = keep.tile([P, PAIR, OUT_F], F32, name="e%d" % h)
+            nc.scalar.activation(out=e_h[:], in_=z_h[:], func=ACT.Exp)
+            z.append(z_h)
+            e.append(e_h)
+        for h in range(TILES // PAIR):
+            r = keep.tile([P, PAIR, OUT_F], F32, name="r%d" % h)
+            nc.vector.tensor_scalar(out=r[:], in0=z[h][:], scalar1=0.0, scalar2=-1.0, op0=ALU.max, op1=ALU.add)
+            res = keep.tile([P, PAIR, OUT_F], F32, name="res%d" % h)
+            nc.vector.scalar_tensor_tensor(
+                out=res[:].rearrange("p b f -> p (b f)"),
+                in0=e[h][:].rearrange("p b f -> p (b f)"),
+                scalar=1.0,
+                in1=r[:].rearrange("p b f -> p (b f)"),
+                op0=ALU.min,
+                op1=ALU.add,
+            )
+            nc.sync.dma_start(out=out_blocks[:, PAIR * h : PAIR * h + PAIR, :], in_=res[:])

@@ -22,6 +22,9 @@ K_PASS = P * PACK
 PASSES = IN_F // K_PASS
 TILES = NODES // P
 
+W_SLOT = 2
+FIRST_PIECES = 2
+
 FLOPS = 2 * NODES * IN_F * OUT_F + 2 * NODES * NODES * OUT_F
 
 
@@ -50,14 +53,17 @@ def tile_netgraphconvolution_s_kernel(tc, x, adj, weight, bias, out):
         for t in range(TILES):
             x_t = keep.tile([P, IN_F], BF16, name="x_rows%d" % t)
             x_rows.append(x_t)
-        nc.sync.dma_start(out=x_rows[0][:], in_=x_tiles[0, 0])
+        for t in range(TILES):
+            pieces = FIRST_PIECES if t == 0 else 1
+            width = IN_F // pieces
+            for c in range(pieces):
+                cols = slice(c * width, (c + 1) * width)
+                nc.sync.dma_start(out=x_rows[t][:, cols], in_=x_tiles[t // PAIR, t % PAIR][:, cols])
         w_raw = keep.tile([P, PASSES, PACK, OUT_F], BF16)
         nc.sync.dma_start(
             out=w_raw[:].rearrange("p g (u e) c -> p (g u) (e c)", u=HALVES),
             in_=weight.rearrange("(g u p e) c -> p (g u) (e c)", g=PASSES, u=HALVES, p=P),
         )
-        for t in range(1, TILES):
-            nc.sync.dma_start(out=x_rows[t][:], in_=x_tiles[t // PAIR, t % PAIR])
         adj_blocks = adj.rearrange("(p b) j -> p b j", b=TILES)
         adj_rows = []
         for h in range(TILES // PAIR):
@@ -66,14 +72,16 @@ def tile_netgraphconvolution_s_kernel(tc, x, adj, weight, bias, out):
             adj_rows.append(adj_h)
 
         w_grouped = keep.tile([P, PASSES, OUT_F, PACK], BF16, align_bytes=64)
-        nc.vector.tensor_copy(out=w_grouped[:], in_=w_raw[:].rearrange("p g t c -> p g c t"))
         w_codes = keep.tile([P, PASSES, OUT_F], U32, align_bytes=64)
         w_scales = keep.tile([P, PASSES, OUT_F], U8, align_bytes=64)
-        nc.vector.quantize_mx(
-            out=w_codes[:].rearrange("p g c -> p (g c)").bitcast(FP8X4),
-            scales=w_scales[:].rearrange("p g c -> p (g c)"),
-            in_=w_grouped[:].rearrange("p g c t -> p (g c t)"),
-        )
+
+        def quantise_weight():
+            nc.vector.tensor_copy(out=w_grouped[:], in_=w_raw[:].rearrange("p g t c -> p g c t"))
+            nc.vector.quantize_mx(
+                out=w_codes[:].rearrange("p g c -> p (g c)").bitcast(FP8X4),
+                scales=w_scales[:].rearrange("p g c -> p (g c)"),
+                in_=w_grouped[:].rearrange("p g c t -> p (g c t)"),
+            )
 
         x_codes = keep.tile([P, TILES, PASSES, P], U32, align_bytes=64)
         x_scales = keep.tile([P, TILES, PASSES, P], U8, align_bytes=64)
@@ -89,10 +97,7 @@ def tile_netgraphconvolution_s_kernel(tc, x, adj, weight, bias, out):
                 nc.tensor.transpose(xT[:, q, :], x_words[:, P * q : P * q + P], ident[:])
             grouped_words = x_grouped[t][:].bitcast(F32).rearrange("p (g n u) -> p g n u", g=PASSES, u=HALVES)
             turned_words = xT[:].rearrange("p (g u) n -> p g n u", g=PASSES)
-            if t % 2 == 0:
-                nc.scalar.copy(out=grouped_words, in_=turned_words)
-            else:
-                nc.vector.tensor_copy(out=grouped_words, in_=turned_words)
+            nc.scalar.copy(out=grouped_words, in_=turned_words)
 
         def quantise_x(t):
             nc.vector.quantize_mx(
@@ -101,42 +106,35 @@ def tile_netgraphconvolution_s_kernel(tc, x, adj, weight, bias, out):
                 in_=x_grouped[t][:],
             )
 
-        turn_x(0)
-        for t in range(1, TILES):
+        for t in range(TILES):
             turn_x(t)
-            quantise_x(t - 1)
-        quantise_x(TILES - 1)
+            if t == W_SLOT:
+                quantise_weight()
+            quantise_x(t)
 
         a_codes = keep.tile([P, TILES, P], U32, align_bytes=64)
         a_scales = keep.tile([P, TILES, P], U8, align_bytes=64)
         adj_turned = []
-        for h in range(TILES // PAIR):
-            aT = turned.tile([P, PAIR, HALVES, P], F32, tag="turned")
-            for s in range(PAIR):
-                adj_words = adj_rows[h][:, s, :].bitcast(F32)
-                for u in range(HALVES):
-                    nc.tensor.transpose(aT[:, s, u, :], adj_words[:, P * u : P * u + P], ident[:])
+        for b in range(TILES):
+            aT = turned.tile([P, HALVES, P], F32, tag="turned")
+            adj_words = adj_rows[b // PAIR][:, b % PAIR, :].bitcast(F32)
+            for u in range(HALVES):
+                nc.tensor.transpose(aT[:, u, :], adj_words[:, P * u : P * u + P], ident[:])
             adj_turned.append(aT)
 
-        def square_and_quantise(h):
-            a_grouped = keep.tile([P, PAIR, P * PACK], BF16, name="a_grouped%d" % h, align_bytes=64)
-            for s in range(PAIR):
-                nc.scalar.activation(
-                    out=a_grouped[:, s, :].rearrange("p (i u e) -> p i u e", u=HALVES, e=PAIR),
-                    in_=adj_turned[h][:, s].bitcast(BF16).rearrange("p u (i e) -> p i u e", e=PAIR),
-                    func=ACT.Square,
-                )
+        def square_and_quantise(b):
+            a_grouped = keep.tile([P, P * PACK], BF16, name="a_grouped%d" % b, align_bytes=64)
+            nc.scalar.activation(
+                out=a_grouped[:].rearrange("p (i u e) -> p i u e", u=HALVES, e=PAIR),
+                in_=adj_turned[b][:].bitcast(BF16).rearrange("p u (i e) -> p i u e", e=PAIR),
+                func=ACT.Square,
+            )
             nc.vector.quantize_mx(
-                out=a_codes[:, PAIR * h : PAIR * h + PAIR, :].rearrange("p s i -> p (s i)").bitcast(FP8X4),
-                scales=a_scales[:, PAIR * h : PAIR * h + PAIR, :].rearrange("p s i -> p (s i)"),
-                in_=a_grouped[:].rearrange("p s c -> p (s c)"),
+                out=a_codes[:, b, :].bitcast(FP8X4), scales=a_scales[:, b, :], in_=a_grouped[:]
             )
 
-        bias_ps = sums.tile([P, OUT_F], F32)
-        nc.tensor.matmul(out=bias_ps[:], lhsT=ones[:], rhs=bias_rows[:], start=True, stop=True)
-        bias_all = keep.tile([P, OUT_F], F32)
-
         square_and_quantise(0)
+        square_and_quantise(1)
 
         sup_ps = sums.tile([P, TILES, OUT_F], F32)
         for t in range(TILES):
@@ -150,6 +148,9 @@ def tile_netgraphconvolution_s_kernel(tc, x, adj, weight, bias, out):
                     start=(g == 0),
                     stop=(g == PASSES - 1),
                 )
+        bias_ps = sums.tile([P, OUT_F], F32)
+        nc.tensor.matmul(out=bias_ps[:], lhsT=ones[:], rhs=bias_rows[:], start=True, stop=True)
+        bias_all = keep.tile([P, OUT_F], F32)
         sup_grouped = keep.tile([P, OUT_F, PACK], BF16, align_bytes=64)
         nc.vector.tensor_copy(out=sup_grouped[:], in_=sup_ps[:].rearrange("p t f -> p f t"))
         sup_codes = keep.tile([P, OUT_F], U32, align_bytes=64)
@@ -160,7 +161,8 @@ def tile_netgraphconvolution_s_kernel(tc, x, adj, weight, bias, out):
             in_=sup_grouped[:].rearrange("p f t -> p (f t)"),
         )
 
-        square_and_quantise(1)
+        square_and_quantise(2)
+        square_and_quantise(3)
         nc.scalar.copy(out=bias_all[:], in_=bias_ps[:])
 
         out_blocks = out.rearrange("(p b) f -> p b f", b=TILES)

@@ -7,6 +7,7 @@ F32 = mybir.dt.float32
 BF16 = mybir.dt.bfloat16
 U32 = mybir.dt.uint32
 U8 = mybir.dt.uint8
+I32 = mybir.dt.int32
 FP8X4 = mybir.dt.float8_e4m3fn_x4
 ACT = mybir.ActivationFunctionType
 ALU = mybir.AluOpType
@@ -24,6 +25,7 @@ TILES = NODES // P
 
 W_SLOT = 2
 FIRST_PIECES = 2
+IDLE_AT_START = 3
 
 FLOPS = 2 * NODES * IN_F * OUT_F + 2 * NODES * NODES * OUT_F
 
@@ -41,6 +43,28 @@ def tile_netgraphconvolution_s_kernel(tc, x, adj, weight, bias, out):
         warm_in = keep.tile([P, 1], F32)
         warm_out = keep.tile([P, 1], F32)
         nc.vector.memset(warm_in[:], 0.0)
+
+        idle_zeros = keep.tile([P, K_PASS * PACK], BF16, align_bytes=64)
+        nc.vector.memset(idle_zeros[:].bitcast(I32), 0)
+        idle_codes = keep.tile([P, K_PASS], U32, align_bytes=64)
+        idle_scales = keep.tile([P, K_PASS], U8, align_bytes=64)
+        nc.vector.quantize_mx(out=idle_codes[:].bitcast(FP8X4), scales=idle_scales[:], in_=idle_zeros[:])
+        idle_ps = sums.tile([P, K_PASS], F32, tag="out_ps1")
+
+        def idle_pass():
+            nc.tensor.matmul_mx(
+                out=idle_ps[:],
+                lhsT=idle_codes[:, 0:P].bitcast(FP8X4),
+                lhsT_scale=idle_scales[:, 0:P],
+                rhs=idle_codes[:].bitcast(FP8X4),
+                rhs_scale=idle_scales[:],
+                start=True,
+                stop=True,
+            )
+
+        for n in range(IDLE_AT_START):
+            idle_pass()
+
         bias_rows = keep.tile([P, OUT_F], BF16)
         nc.vector.memset(bias_rows[:], 0.0)
         ones = keep.tile([P, P], BF16)
@@ -108,6 +132,8 @@ def tile_netgraphconvolution_s_kernel(tc, x, adj, weight, bias, out):
 
         for t in range(TILES):
             turn_x(t)
+            if t % 2 == 1:
+                idle_pass()
             if t == W_SLOT:
                 quantise_weight()
             quantise_x(t)
@@ -169,7 +195,7 @@ def tile_netgraphconvolution_s_kernel(tc, x, adj, weight, bias, out):
         z = []
         e = []
         for h in range(TILES // PAIR):
-            out_ps = sums.tile([P, PAIR, OUT_F], F32, name="out_ps%d" % h)
+            out_ps = sums.tile([P, PAIR, OUT_F], F32, name="out_ps%d" % h, tag="out_ps%d" % h)
             for s in range(PAIR):
                 b = PAIR * h + s
                 nc.tensor.matmul_mx(

from contextlib import ExitStack

import concourse.mybir as mybir
from concourse.masks import make_identity

F32 = mybir.dt.float32
BF16 = mybir.dt.bfloat16
U32 = mybir.dt.uint32
U8 = mybir.dt.uint8
I32 = mybir.dt.int32
FP8X4 = mybir.dt.float8_e4m3fn_x4
ACT = mybir.ActivationFunctionType
ALU = mybir.AluOpType

P = 128
PACK = 4
HALVES = 2
PAIR = 2
NODES = 512
IN_F = 1024
OUT_F = 128
K_PASS = P * PACK
PASSES = IN_F // K_PASS
TILES = NODES // P

W_SLOT = 2
FIRST_PIECES = 2
IDLE_AT_START = 3

FLOPS = 2 * NODES * IN_F * OUT_F + 2 * NODES * NODES * OUT_F


def tile_netgraphconvolution_s_kernel(tc, x, adj, weight, bias, out):
    nc = tc.nc
    with ExitStack() as ctx:
        keep = ctx.enter_context(tc.tile_pool(name="keep", bufs=1))
        turned = ctx.enter_context(tc.psum_pool(name="turned", bufs=4))
        sums = ctx.enter_context(tc.psum_pool(name="sums", bufs=1))
        ctx.enter_context(tc.manual_schedule())

        ident = keep.tile([P, P], F32)
        make_identity(nc, ident[:])
        warm_in = keep.tile([P, 1], F32)
        warm_out = keep.tile([P, 1], F32)
        nc.vector.memset(warm_in[:], 0.0)

        idle_zeros = keep.tile([P, K_PASS * PACK], BF16, align_bytes=64)
        nc.vector.memset(idle_zeros[:].bitcast(I32), 0)
        idle_codes = keep.tile([P, K_PASS], U32, align_bytes=64)
        idle_scales = keep.tile([P, K_PASS], U8, align_bytes=64)
        nc.vector.quantize_mx(out=idle_codes[:].bitcast(FP8X4), scales=idle_scales[:], in_=idle_zeros[:])
        idle_ps = sums.tile([P, K_PASS], F32, tag="out_ps1")

        def idle_pass():
            nc.tensor.matmul_mx(
                out=idle_ps[:],
                lhsT=idle_codes[:, 0:P].bitcast(FP8X4),
                lhsT_scale=idle_scales[:, 0:P],
                rhs=idle_codes[:].bitcast(FP8X4),
                rhs_scale=idle_scales[:],
                start=True,
                stop=True,
            )

        for n in range(IDLE_AT_START):
            idle_pass()

        bias_rows = keep.tile([P, OUT_F], BF16)
        nc.vector.memset(bias_rows[:], 0.0)
        ones = keep.tile([P, P], BF16)
        nc.vector.memset(ones[:], 1.0)
        nc.scalar.dma_start(out=bias_rows[0:1, :], in_=bias.rearrange("(o f) -> o f", o=1))
        nc.scalar.activation(out=warm_out[:], in_=warm_in[:], func=ACT.Exp)

        x_tiles = x.rearrange("(u p e) k -> u e p k", u=HALVES, p=P)
        x_rows = []
        for t in range(TILES):
            x_t = keep.tile([P, IN_F], BF16, name="x_rows%d" % t)
            x_rows.append(x_t)
        for t in range(TILES):
            pieces = FIRST_PIECES if t == 0 else 1
            width = IN_F // pieces
            for c in range(pieces):
                cols = slice(c * width, (c + 1) * width)
                nc.sync.dma_start(out=x_rows[t][:, cols], in_=x_tiles[t // PAIR, t % PAIR][:, cols])
        w_raw = keep.tile([P, PASSES, PACK, OUT_F], BF16)
        nc.sync.dma_start(
            out=w_raw[:].rearrange("p g (u e) c -> p (g u) (e c)", u=HALVES),
            in_=weight.rearrange("(g u p e) c -> p (g u) (e c)", g=PASSES, u=HALVES, p=P),
        )
        adj_blocks = adj.rearrange("(p b) j -> p b j", b=TILES)
        adj_rows = []
        for h in range(TILES // PAIR):
            adj_h = keep.tile([P, PAIR, NODES], BF16, name="adj_rows%d" % h)
            nc.sync.dma_start(out=adj_h[:], in_=adj_blocks[:, PAIR * h : PAIR * h + PAIR, :])
            adj_rows.append(adj_h)

        w_grouped = keep.tile([P, PASSES, OUT_F, PACK], BF16, align_bytes=64)
        w_codes = keep.tile([P, PASSES, OUT_F], U32, align_bytes=64)
        w_scales = keep.tile([P, PASSES, OUT_F], U8, align_bytes=64)

        def quantise_weight():
            nc.vector.tensor_copy(out=w_grouped[:], in_=w_raw[:].rearrange("p g t c -> p g c t"))
            nc.vector.quantize_mx(
                out=w_codes[:].rearrange("p g c -> p (g c)").bitcast(FP8X4),
                scales=w_scales[:].rearrange("p g c -> p (g c)"),
                in_=w_grouped[:].rearrange("p g c t -> p (g c t)"),
            )

        x_codes = keep.tile([P, TILES, PASSES, P], U32, align_bytes=64)
        x_scales = keep.tile([P, TILES, PASSES, P], U8, align_bytes=64)
        x_grouped = []
        for t in range(TILES):
            x_g = keep.tile([P, PASSES * P * PACK], BF16, name="x_grouped%d" % t, align_bytes=64)
            x_grouped.append(x_g)

        def turn_x(t):
            x_words = x_rows[t][:].bitcast(F32)
            xT = turned.tile([P, PASSES * HALVES, P], F32, tag="turned")
            for q in range(PASSES * HALVES):
                nc.tensor.transpose(xT[:, q, :], x_words[:, P * q : P * q + P], ident[:])
            grouped_words = x_grouped[t][:].bitcast(F32).rearrange("p (g n u) -> p g n u", g=PASSES, u=HALVES)
            turned_words = xT[:].rearrange("p (g u) n -> p g n u", g=PASSES)
            nc.scalar.copy(out=grouped_words, in_=turned_words)

        def quantise_x(t):
            nc.vector.quantize_mx(
                out=x_codes[:, t].rearrange("p g n -> p (g n)").bitcast(FP8X4),
                scales=x_scales[:, t].rearrange("p g n -> p (g n)"),
                in_=x_grouped[t][:],
            )

        for t in range(TILES):
            turn_x(t)
            if t % 2 == 1:
                idle_pass()
            if t == W_SLOT:
                quantise_weight()
            quantise_x(t)

        a_codes = keep.tile([P, TILES, P], U32, align_bytes=64)
        a_scales = keep.tile([P, TILES, P], U8, align_bytes=64)
        adj_turned = []
        for b in range(TILES):
            aT = turned.tile([P, HALVES, P], F32, tag="turned")
            adj_words = adj_rows[b // PAIR][:, b % PAIR, :].bitcast(F32)
            for u in range(HALVES):
                nc.tensor.transpose(aT[:, u, :], adj_words[:, P * u : P * u + P], ident[:])
            adj_turned.append(aT)

        def square_and_quantise(b):
            a_grouped = keep.tile([P, P * PACK], BF16, name="a_grouped%d" % b, align_bytes=64)
            nc.scalar.activation(
                out=a_grouped[:].rearrange("p (i u e) -> p i u e", u=HALVES, e=PAIR),
                in_=adj_turned[b][:].bitcast(BF16).rearrange("p u (i e) -> p i u e", e=PAIR),
                func=ACT.Square,
            )
            nc.vector.quantize_mx(
                out=a_codes[:, b, :].bitcast(FP8X4), scales=a_scales[:, b, :], in_=a_grouped[:]
            )

        square_and_quantise(0)
        square_and_quantise(1)

        sup_ps = sums.tile([P, TILES, OUT_F], F32)
        for t in range(TILES):
            for g in range(PASSES):
                nc.tensor.matmul_mx(
                    out=sup_ps[:, t, :],
                    lhsT=x_codes[:, t, g, :].bitcast(FP8X4),
                    lhsT_scale=x_scales[:, t, g, :],
                    rhs=w_codes[:, g, :].bitcast(FP8X4),
                    rhs_scale=w_scales[:, g, :],
                    start=(g == 0),
                    stop=(g == PASSES - 1),
                )
        bias_ps = sums.tile([P, OUT_F], F32)
        nc.tensor.matmul(out=bias_ps[:], lhsT=ones[:], rhs=bias_rows[:], start=True, stop=True)
        bias_all = keep.tile([P, OUT_F], F32)
        sup_grouped = keep.tile([P, OUT_F, PACK], BF16, align_bytes=64)
        nc.vector.tensor_copy(out=sup_grouped[:], in_=sup_ps[:].rearrange("p t f -> p f t"))
        sup_codes = keep.tile([P, OUT_F], U32, align_bytes=64)
        sup_scales = keep.tile([P, OUT_F], U8, align_bytes=64)
        nc.vector.quantize_mx(
            out=sup_codes[:].bitcast(FP8X4),
            scales=sup_scales[:],
            in_=sup_grouped[:].rearrange("p f t -> p (f t)"),
        )

        square_and_quantise(2)
        square_and_quantise(3)
        nc.scalar.copy(out=bias_all[:], in_=bias_ps[:])

        out_blocks = out.rearrange("(p b) f -> p b f", b=TILES)
        z = []
        e = []
        for h in range(TILES // PAIR):
            out_ps = sums.tile([P, PAIR, OUT_F], F32, name="out_ps%d" % h, tag="out_ps%d" % h)
            for s in range(PAIR):
                b = PAIR * h + s
                nc.tensor.matmul_mx(
                    out=out_ps[:, s, :],
                    lhsT=a_codes[:, b, :].bitcast(FP8X4),
                    lhsT_scale=a_scales[:, b, :],
                    rhs=sup_codes[:].bitcast(FP8X4),
                    rhs_scale=sup_scales[:],
                    start=True,
                    stop=True,
                )
            z_h = keep.tile([P, PAIR, OUT_F], F32, name="z%d" % h)
            nc.vector.tensor_tensor(
                out=z_h[:], in0=out_ps[:], in1=bias_all[:].unsqueeze(1).to_broadcast([P, PAIR, OUT_F]), op=ALU.add
            )
            e_h = keep.tile([P, PAIR, OUT_F], F32, name="e%d" % h)
            nc.scalar.activation(out=e_h[:], in_=z_h[:], func=ACT.Exp)
            z.append(z_h)
            e.append(e_h)
        for h in range(TILES // PAIR):
            r = keep.tile([P, PAIR, OUT_F], F32, name="r%d" % h)
            nc.vector.tensor_scalar(out=r[:], in0=z[h][:], scalar1=0.0, scalar2=-1.0, op0=ALU.max, op1=ALU.add)
            res = keep.tile([P, PAIR, OUT_F], F32, name="res%d" % h)
            nc.vector.scalar_tensor_tensor(
                out=res[:].rearrange("p b f -> p (b f)"),
                in0=e[h][:].rearrange("p b f -> p (b f)"),
                scalar=1.0,
                in1=r[:].rearrange("p b f -> p (b f)"),
                op0=ALU.min,
                op1=ALU.add,
            )
            nc.sync.dma_start(out=out_blocks[:, PAIR * h : PAIR * h + PAIR, :], in_=res[:])
